import numpy as np
import ml_dtypes


def mxq(x, axis, fmt="e4m3"):
    dtype, down = {"e4m3": (ml_dtypes.float8_e4m3fn, 7), "e5m2": (ml_dtypes.float8_e5m2, 14)}[fmt]
    v = np.moveaxis(np.asarray(x, np.float32).astype(ml_dtypes.bfloat16).astype(np.float64), axis, -1)
    blocks = v.reshape(v.shape[:-1] + (-1, 32))
    amax = np.abs(blocks).max(-1, keepdims=True)
    byte = np.maximum(np.where(amax > 0, np.frexp(amax)[1] - 1 + 127, 0) - down, 1)
    scale = np.exp2(byte - 127.0)
    codes = (blocks / scale).astype(np.float32).astype(dtype).astype(np.float64)
    return np.moveaxis((codes * scale).reshape(v.shape), -1, axis)


WIDE = False


def mx_kscale(k):
    if not WIDE:
        return np.ones(k)
    levels = np.array([10, -10, 5, -5, 0])
    a = np.random.permutation(np.resize(levels, k // 512 * 4)).reshape(k // 512, 4)
    idx = np.arange(k)
    return np.exp2(a[idx // 512, idx % 128 // 32])


BF16 = ml_dtypes.bfloat16


def bf(x):
    return np.asarray(x, np.float32).astype(BF16)


def f64(x):
    return np.asarray(x).astype(np.float64)


E2M1 = np.array([0.0, 0.5, 1.0, 1.5, 2.0, 3.0, 4.0, 6.0, -0.0, -0.5, -1.0, -1.5, -2.0, -3.0, -4.0, -6.0])


def pack_weight(w, fmt):
    k, n = w.shape
    w = f64(bf(w)).reshape(k // 32, 32, n)
    amax = np.abs(w).max(1)
    if fmt == "e4m3":
        byte = np.frexp(amax)[1] - 1 + 127 - 7
    else:
        mant, ex = np.frexp(amax / 6.0)
        byte = np.where(mant > 0.5, ex, ex - 1) + 127
    byte = np.clip(np.where(amax > 0, byte, 1), 1, 254)
    scaled = (w * np.exp2(127.0 - byte)[:, None, :]).reshape(k, n).astype(np.float32)
    by_word = np.ascontiguousarray(scaled.reshape(k // 512, 128, 4, n).transpose(0, 1, 3, 2))
    if fmt == "e4m3":
        words = by_word.astype(ml_dtypes.float8_e4m3fn).view(np.uint8)
    else:
        c = by_word.astype(ml_dtypes.float4_e2m1fn).view(np.uint8) & 0xF
        words = c[..., 0::2] | (c[..., 1::2] << 4)
    return np.ascontiguousarray(words), np.ascontiguousarray(byte.astype(np.uint8).reshape(k // 512, 16, n))


def unpack_weight(words, scales, fmt):
    g, p, n, _ = words.shape
    if fmt == "e4m3":
        vals = np.ascontiguousarray(words).view(ml_dtypes.float8_e4m3fn).astype(np.float64)
    else:
        nib = np.empty((g, p, n, 4), np.uint8)
        nib[..., 0::2] = words & 0xF
        nib[..., 1::2] = words >> 4
        vals = E2M1[nib]
    vals = vals * np.repeat(np.exp2(scales.astype(np.float64) - 127.0), 8, axis=1)[..., None]
    return vals.transpose(0, 1, 3, 2).reshape(g * 512, n)


B, N, F, G, K = 4, 128, 16384, 512, 2048
EPS = 1e-8


def setup_inputs():
    s = mx_kscale(F)
    a = np.random.standard_normal((B, N, 1))
    g = np.random.standard_normal((B, 1, F))
    h = 2.0 * (np.random.standard_normal((B, N, F)) + a * g)
    w = (np.random.standard_normal((F, G)) + 0.5 * np.random.standard_normal((F, 1))) / np.sqrt(F)
    words, scales = pack_weight(w / s[:, None], "e4m3")
    return {"h": bf(h * s), "W_h_words": words, "W_h_scales": scales, "beta": bf(2.0 + np.random.uniform(size=1))}


def reference(h, W_h_words, W_h_scales, beta):
    Wh = mxq(f64(h), 2, "e4m3") @ unpack_weight(W_h_words, W_h_scales, "e4m3")
    xm = Wh - Wh.mean(-1, keepdims=True)
    xq = mxq(xm, 2, "e4m3")
    cov = xq @ xq.transpose(0, 2, 1)
    norm = np.sqrt((xm * xm).sum(-1))
    denom = norm[:, :, None] * norm[:, None, :] + EPS
    return f64(beta) * np.abs(cov / denom)

@@ -1,0 +1,217 @@
+from contextlib import ExitStack
+
+import concourse.mybir as mybir
+from concourse.masks import make_identity
+
+F32 = mybir.dt.float32
+BF16 = mybir.dt.bfloat16
+I32 = mybir.dt.int32
+U32 = mybir.dt.uint32
+U8 = mybir.dt.uint8
+FP8X4 = mybir.dt.float8_e4m3fn_x4
+ACT = mybir.ActivationFunctionType
+ALU = mybir.AluOpType
+
+P = 128
+PACK = 4
+K_PASS = P * PACK
+GRAPHS = 4
+F_IN = 16384
+F_OUT = 512
+EPS = 1e-8
+
+PASSES = F_IN // K_PASS
+CHUNK = 8
+CHUNKS = PASSES // CHUNK
+UNITS = CHUNKS * GRAPHS
+PAIRS = 2
+BANK_PASSES = 2
+PLANES = 4
+LOAD_LEAD = 3
+
+FLOPS = 2 * GRAPHS * P * F_IN * F_OUT + 2 * GRAPHS * P * P * F_OUT
+
+
+def tile_pearsonattention_pa_k_kernel(tc, h, W_h_words, W_h_scales, beta, out):
+    nc = tc.nc
+    w_words_dram = W_h_words.rearrange("g p n t -> p g (n t)").bitcast(I32)
+    w_scales_dram = W_h_scales.bitcast(I32)
+
+    with ExitStack() as ctx:
+        const = ctx.enter_context(tc.tile_pool(name="const", bufs=1))
+        h_pool = ctx.enter_context(tc.tile_pool(name="h_pool", bufs=LOAD_LEAD + 1))
+        w_pool = ctx.enter_context(tc.tile_pool(name="w_pool", bufs=2))
+        work = ctx.enter_context(tc.tile_pool(name="work", bufs=2))
+        per_graph = ctx.enter_context(tc.tile_pool(name="per_graph", bufs=GRAPHS))
+        sums = ctx.enter_context(tc.psum_pool(name="sums", bufs=1))
+        flips = ctx.enter_context(tc.psum_pool(name="flips", bufs=4))
+        ctx.enter_context(tc.manual_schedule())
+
+        beta_bf = const.tile([P, 1], BF16, name="beta_bf")
+        nc.scalar.dma_start(out=beta_bf[:], in_=beta.partition_broadcast(P))
+        ident_f32 = const.tile([P, P], F32, name="ident_f32")
+        make_identity(nc, ident_f32[:])
+        ident_bf = const.tile([P, P], BF16, name="ident_bf")
+        make_identity(nc, ident_bf[:])
+        w_planes = const.tile([P, PASSES // PLANES, F_OUT], U8, name="w_planes", align_bytes=64)
+        nc.vector.memset(w_planes[:].bitcast(I32), 0)
+        one = const.tile([P, 1], F32, name="one")
+        nc.vector.memset(one[:], 1.0)
+        warm = const.tile([P, 1], F32, name="warm")
+        nc.scalar.activation(out=warm[:], in_=one[:], func=ACT.Sqrt)
+        beta_f32 = const.tile([P, 1], F32, name="beta_f32")
+        nc.vector.tensor_copy(out=beta_f32[:], in_=beta_bf[:])
+
+        acc = [sums.tile([P, F_OUT], F32, name="acc%d" % b) for b in range(GRAPHS)]
+
+        raw = {}
+        weights = {}
+        ordered = {}
+        codes = {}
+        planes = {}
+        graph = [{} for b in range(GRAPHS)]
+
+        def load(u):
+            c, b = divmod(u, GRAPHS)
+            raw[u] = h_pool.tile([P, CHUNK * K_PASS], BF16, name="h_raw")
+            nc.sync.dma_start(out=raw[u][:], in_=h[b, :, c * CHUNK * K_PASS : (c + 1) * CHUNK * K_PASS])
+            if b != 1:
+                return
+            for tile_no in range(c * CHUNK // PLANES, (c + 1) * CHUNK // PLANES):
+                for quad in range(4):
+                    nc.sync.dma_start(
+                        out=w_planes[32 * quad : 32 * quad + 4 * PLANES, tile_no, :].bitcast(I32),
+                        in_=w_scales_dram[PLANES * tile_no : PLANES * (tile_no + 1), 4 * quad : 4 * quad + 4, :],
+                    )
+            weights[c] = w_pool.tile([P, CHUNK, F_OUT], U32, name="w_words", align_bytes=64)
+            for half in range(2):
+                g0 = half * CHUNK // 2
+                nc.sync.dma_start(
+                    out=weights[c][:, g0 : g0 + CHUNK // 2, :].bitcast(I32),
+                    in_=w_words_dram[:, c * CHUNK + g0 : c * CHUNK + g0 + CHUNK // 2, :],
+                )
+
+        def sort_words(u):
+            ordered[u] = work.tile([P, CHUNK, PAIRS, P], F32, name="h_sorted")
+            nc.vector.tensor_copy(
+                out=ordered[u][:],
+                in_=raw[u][:].bitcast(F32).rearrange("n (g p i) -> n g i p", g=CHUNK, i=PAIRS),
+            )
+
+        def flip_and_quantise(u):
+            grouped = work.tile([P, CHUNK * K_PASS], BF16, name="h_grouped", align_bytes=64)
+            grouped_words = grouped[:].bitcast(F32).rearrange("p (g n i) -> p g n i", g=CHUNK, i=PAIRS)
+            codes[u] = work.tile([P, CHUNK * P], U32, name="h_codes", align_bytes=64, bufs=3)
+            planes[u] = work.tile([P, CHUNK * P], U8, name="h_planes", align_bytes=64, bufs=3)
+            for bank in range(CHUNK // BANK_PASSES):
+                g0 = bank * BANK_PASSES
+                flipped = flips.tile([P, BANK_PASSES, PAIRS, P], F32, name="flipped", tag="flip")
+                for g in range(BANK_PASSES):
+                    for i in range(PAIRS):
+                        nc.tensor.transpose(flipped[:, g, i, :], ordered[u][:, g0 + g, i, :], ident_f32[:])
+                nc.scalar.copy(
+                    out=grouped_words[:, g0 : g0 + BANK_PASSES, :, :],
+                    in_=flipped[:].rearrange("p g i n -> p g n i"),
+                )
+            for half in range(2):
+                cols = slice(half * CHUNK * P // 2, (half + 1) * CHUNK * P // 2)
+                nc.vector.quantize_mx(
+                    out=codes[u][:, cols].bitcast(FP8X4),
+                    scales=planes[u][:, cols],
+                    in_=grouped[:, half * CHUNK * K_PASS // 2 : (half + 1) * CHUNK * K_PASS // 2],
+                )
+
+        def project(u):
+            c, b = divmod(u, GRAPHS)
+            for g in range(CHUNK):
+                tile_no, j = divmod(c * CHUNK + g, PLANES)
+                nc.tensor.matmul_mx(
+                    out=acc[b][:],
+                    lhsT=codes[u][:, g * P : (g + 1) * P].bitcast(FP8X4),
+                    lhsT_scale=planes[u][:, g * P : (g + 1) * P],
+                    rhs=weights[c][:, g, :].bitcast(FP8X4),
+                    rhs_scale=w_planes[4 * j : P, tile_no, :],
+                    start=(c == 0 and g == 0),
+                    stop=(c == CHUNKS - 1 and g == CHUNK - 1),
+                )
+
+        def centre(b):
+            t = graph[b]
+            stats = per_graph.tile([P, 6], F32, name="stats")
+            nc.vector.bn_stats(out=stats[:], in_=acc[b][:])
+            mean_var = per_graph.tile([P, 2], F32, name="mean_var")
+            nc.vector.bn_aggr(out=mean_var[:], in_=stats[:])
+            t["xm"] = per_graph.tile([P, PACK, P], BF16, name="xm")
+            nc.vector.tensor_scalar(
+                out=t["xm"][:],
+                in0=acc[b][:].rearrange("n (j t) -> n t j", t=PACK),
+                scalar1=mean_var[:, 0:1],
+                scalar2=None,
+                op0=ALU.subtract,
+            )
+            t["norm"] = per_graph.tile([P, 1], F32, name="norm")
+            nc.scalar.activation(out=t["norm"][:], in_=mean_var[:, 1:2], func=ACT.Sqrt, scale=float(F_OUT))
+
+        def flip_xm(b):
+            t = graph[b]
+            xm_flipped = sums.tile([P, PACK, P], BF16, name="xm_flipped", tag="acc%d" % b)
+            for k in range(PACK):
+                nc.tensor.transpose(xm_flipped[:, k, :], t["xm"][:, k, :], ident_bf[:])
+            norm_row = flips.tile([P, P], F32, name="norm_row", tag="flip")
+            nc.tensor.matmul(
+                out=norm_row[:], lhsT=t["norm"][:, 0:1].to_broadcast([P, P]), rhs=ident_f32[:], start=True, stop=True
+            )
+            xm_grouped = per_graph.tile([P, P, PACK], BF16, name="xm_grouped", align_bytes=64)
+            nc.scalar.copy(out=xm_grouped[:], in_=xm_flipped[:].rearrange("j t n -> j n t"))
+            t["codes"] = per_graph.tile([P, P], U32, name="xm_codes", align_bytes=64)
+            t["plane"] = per_graph.tile([P, P], U8, name="xm_plane", align_bytes=64)
+            nc.vector.quantize_mx(
+                out=t["codes"][:].bitcast(FP8X4),
+                scales=t["plane"][:],
+                in_=xm_grouped[:].rearrange("j n t -> j (n t)"),
+            )
+            denom = per_graph.tile([P, P], F32, name="denom")
+            nc.vector.tensor_scalar(
+                out=denom[:], in0=norm_row[:], scalar1=t["norm"][:, 0:1], scalar2=EPS, op0=ALU.mult, op1=ALU.add
+            )
+            t["recip"] = per_graph.tile([P, P], F32, name="recip")
+            nc.vector.reciprocal(out=t["recip"][:], in_=denom[:])
+
+        def correlate(b):
+            t = graph[b]
+            cov = sums.tile([P, P], F32, name="cov", tag="acc%d" % b)
+            nc.tensor.matmul_mx(
+                out=cov[:],
+                lhsT=t["codes"][:].bitcast(FP8X4),
+                lhsT_scale=t["plane"][:],
+                rhs=t["codes"][:].bitcast(FP8X4),
+                rhs_scale=t["plane"][:],
+                start=True,
+                stop=True,
+            )
+            cov_abs = per_graph.tile([P, P], F32, name="cov_abs")
+            nc.scalar.activation(out=cov_abs[:], in_=cov[:], func=ACT.Abs)
+            result = per_graph.tile([P, P], F32, name="result")
+            nc.vector.scalar_tensor_tensor(
+                out=result[:], in0=cov_abs[:], scalar=beta_f32[:, 0:1], in1=t["recip"][:], op0=ALU.mult, op1=ALU.mult
+            )
+            nc.sync.dma_start(out=out[b], in_=result[:])
+
+        first_last = UNITS - GRAPHS
+        for step in range(UNITS + LOAD_LEAD + 5):
+            if step < UNITS:
+                load(step)
+            u = step - LOAD_LEAD
+            if 0 <= u < UNITS:
+                sort_words(u)
+            if 0 <= u - 1 < UNITS:
+                flip_and_quantise(u - 1)
+            m = u - 2
+            if 0 <= m - 2 - first_last < GRAPHS:
+                flip_xm(m - 2 - first_last)
+            if 0 <= m - 3 - first_last < GRAPHS:
+                correlate(m - 3 - first_last)
+            if 0 <= m < UNITS:
+                project(m)
+            if 0 <= m - first_last < GRAPHS:
+                centre(m - first_last)

@@ -21,13 +21,19 @@ F_OUT = 512
 EPS = 1e-8
 
 PASSES = F_IN // K_PASS
-CHUNK = 8
-CHUNKS = PASSES // CHUNK
+LOAD_PASSES = 8
+CHUNKS = PASSES // LOAD_PASSES
 UNITS = CHUNKS * GRAPHS
+RUN_PASSES = 4
+RUNS_PER_UNIT = LOAD_PASSES // RUN_PASSES
+RUNS = UNITS * RUNS_PER_UNIT
 PAIRS = 2
 BANK_PASSES = 2
 PLANES = 4
 LOAD_LEAD = 3
+FLIP_LAG = 1
+PROJECT_LAG = 2
+EPILOGUE_LAG = 2
 
 FLOPS = 2 * GRAPHS * P * F_IN * F_OUT + 2 * GRAPHS * P * P * F_OUT
 
@@ -73,66 +79,63 @@ def tile_pearsonattention_pa_k_kernel(tc, h, W_h_words, W_h_scales, beta, out):
 
         def load(u):
             c, b = divmod(u, GRAPHS)
-            raw[u] = h_pool.tile([P, CHUNK * K_PASS], BF16, name="h_raw")
-            nc.sync.dma_start(out=raw[u][:], in_=h[b, :, c * CHUNK * K_PASS : (c + 1) * CHUNK * K_PASS])
+            raw[u] = h_pool.tile([P, LOAD_PASSES * K_PASS], BF16, name="h_raw")
+            nc.sync.dma_start(out=raw[u][:], in_=h[b, :, c * LOAD_PASSES * K_PASS : (c + 1) * LOAD_PASSES * K_PASS])
             if b != 1:
                 return
-            for tile_no in range(c * CHUNK // PLANES, (c + 1) * CHUNK // PLANES):
+            for tile_no in range(c * LOAD_PASSES // PLANES, (c + 1) * LOAD_PASSES // PLANES):
                 for quad in range(4):
                     nc.sync.dma_start(
                         out=w_planes[32 * quad : 32 * quad + 4 * PLANES, tile_no, :].bitcast(I32),
                         in_=w_scales_dram[PLANES * tile_no : PLANES * (tile_no + 1), 4 * quad : 4 * quad + 4, :],
                     )
-            weights[c] = w_pool.tile([P, CHUNK, F_OUT], U32, name="w_words", align_bytes=64)
-            for half in range(2):
-                g0 = half * CHUNK // 2
+            weights[c] = w_pool.tile([P, LOAD_PASSES, F_OUT], U32, name="w_words", align_bytes=64)
+            for g0 in range(0, LOAD_PASSES, RUN_PASSES):
                 nc.sync.dma_start(
-                    out=weights[c][:, g0 : g0 + CHUNK // 2, :].bitcast(I32),
-                    in_=w_words_dram[:, c * CHUNK + g0 : c * CHUNK + g0 + CHUNK // 2, :],
+                    out=weights[c][:, g0 : g0 + RUN_PASSES, :].bitcast(I32),
+                    in_=w_words_dram[:, c * LOAD_PASSES + g0 : c * LOAD_PASSES + g0 + RUN_PASSES, :],
                 )
 
-        def sort_words(u):
-            ordered[u] = work.tile([P, CHUNK, PAIRS, P], F32, name="h_sorted")
+        def sort_words(r):
+            u, part = divmod(r, RUNS_PER_UNIT)
+            ordered[r] = work.tile([P, RUN_PASSES, PAIRS, P], F32, name="h_sorted")
             nc.vector.tensor_copy(
-                out=ordered[u][:],
-                in_=raw[u][:].bitcast(F32).rearrange("n (g p i) -> n g i p", g=CHUNK, i=PAIRS),
+                out=ordered[r][:],
+                in_=raw[u][:, part * RUN_PASSES * K_PASS : (part + 1) * RUN_PASSES * K_PASS]
+                .bitcast(F32)
+                .rearrange("n (g p i) -> n g i p", g=RUN_PASSES, i=PAIRS),
             )
 
-        def flip_and_quantise(u):
-            grouped = work.tile([P, CHUNK * K_PASS], BF16, name="h_grouped", align_bytes=64)
-            grouped_words = grouped[:].bitcast(F32).rearrange("p (g n i) -> p g n i", g=CHUNK, i=PAIRS)
-            codes[u] = work.tile([P, CHUNK * P], U32, name="h_codes", align_bytes=64, bufs=3)
-            planes[u] = work.tile([P, CHUNK * P], U8, name="h_planes", align_bytes=64, bufs=3)
-            for bank in range(CHUNK // BANK_PASSES):
-                g0 = bank * BANK_PASSES
+        def flip_and_quantise(r):
+            grouped = work.tile([P, RUN_PASSES * K_PASS], BF16, name="h_grouped", align_bytes=64)
+            grouped_words = grouped[:].bitcast(F32).rearrange("p (g n i) -> p g n i", g=RUN_PASSES, i=PAIRS)
+            for g0 in range(0, RUN_PASSES, BANK_PASSES):
                 flipped = flips.tile([P, BANK_PASSES, PAIRS, P], F32, name="flipped", tag="flip")
                 for g in range(BANK_PASSES):
                     for i in range(PAIRS):
-                        nc.tensor.transpose(flipped[:, g, i, :], ordered[u][:, g0 + g, i, :], ident_f32[:])
+                        nc.tensor.transpose(flipped[:, g, i, :], ordered[r][:, g0 + g, i, :], ident_f32[:])
                 nc.scalar.copy(
                     out=grouped_words[:, g0 : g0 + BANK_PASSES, :, :],
                     in_=flipped[:].rearrange("p g i n -> p g n i"),
                 )
-            for half in range(2):
-                cols = slice(half * CHUNK * P // 2, (half + 1) * CHUNK * P // 2)
-                nc.vector.quantize_mx(
-                    out=codes[u][:, cols].bitcast(FP8X4),
-                    scales=planes[u][:, cols],
-                    in_=grouped[:, half * CHUNK * K_PASS // 2 : (half + 1) * CHUNK * K_PASS // 2],
-                )
+            codes[r] = work.tile([P, RUN_PASSES * P], U32, name="h_codes", align_bytes=64, bufs=PROJECT_LAG + 2)
+            planes[r] = work.tile([P, RUN_PASSES * P], U8, name="h_planes", align_bytes=64, bufs=PROJECT_LAG + 2)
+            nc.vector.quantize_mx(out=codes[r][:].bitcast(FP8X4), scales=planes[r][:], in_=grouped[:])
 
-        def project(u):
+        def project(r):
+            u, part = divmod(r, RUNS_PER_UNIT)
             c, b = divmod(u, GRAPHS)
-            for g in range(CHUNK):
-                tile_no, j = divmod(c * CHUNK + g, PLANES)
+            for g in range(RUN_PASSES):
+                in_chunk = part * RUN_PASSES + g
+                tile_no, j = divmod(c * LOAD_PASSES + in_chunk, PLANES)
                 nc.tensor.matmul_mx(
                     out=acc[b][:],
-                    lhsT=codes[u][:, g * P : (g + 1) * P].bitcast(FP8X4),
-                    lhsT_scale=planes[u][:, g * P : (g + 1) * P],
-                    rhs=weights[c][:, g, :].bitcast(FP8X4),
+                    lhsT=codes[r][:, g * P : (g + 1) * P].bitcast(FP8X4),
+                    lhsT_scale=planes[r][:, g * P : (g + 1) * P],
+                    rhs=weights[c][:, in_chunk, :].bitcast(FP8X4),
                     rhs_scale=w_planes[4 * j : P, tile_no, :],
-                    start=(c == 0 and g == 0),
-                    stop=(c == CHUNKS - 1 and g == CHUNK - 1),
+                    start=(c == 0 and in_chunk == 0),
+                    stop=(c == CHUNKS - 1 and in_chunk == LOAD_PASSES - 1),
                 )
 
         def centre(b):
@@ -197,21 +200,22 @@ def tile_pearsonattention_pa_k_kernel(tc, h, W_h_words, W_h_scales, beta, out):
             )
             nc.sync.dma_start(out=out[b], in_=result[:])
 
-        first_last = UNITS - GRAPHS
-        for step in range(UNITS + LOAD_LEAD + 5):
-            if step < UNITS:
-                load(step)
-            u = step - LOAD_LEAD
-            if 0 <= u < UNITS:
-                sort_words(u)
-            if 0 <= u - 1 < UNITS:
-                flip_and_quantise(u - 1)
-            m = u - 2
-            if 0 <= m - 2 - first_last < GRAPHS:
-                flip_xm(m - 2 - first_last)
-            if 0 <= m - 3 - first_last < GRAPHS:
-                correlate(m - 3 - first_last)
-            if 0 <= m < UNITS:
+        closing = {(UNITS - GRAPHS + b + 1) * RUNS_PER_UNIT - 1: b for b in range(GRAPHS)}
+        sort_lag = LOAD_LEAD * RUNS_PER_UNIT
+        for step in range(RUNS + sort_lag + FLIP_LAG + PROJECT_LAG + 2 * EPILOGUE_LAG):
+            if step % RUNS_PER_UNIT == 0 and step < RUNS:
+                load(step // RUNS_PER_UNIT)
+            r = step - sort_lag
+            if 0 <= r < RUNS:
+                sort_words(r)
+            if 0 <= r - FLIP_LAG < RUNS:
+                flip_and_quantise(r - FLIP_LAG)
+            m = r - FLIP_LAG - PROJECT_LAG
+            if m - EPILOGUE_LAG in closing:
+                flip_xm(closing[m - EPILOGUE_LAG])
+            if m - 2 * EPILOGUE_LAG in closing:
+                correlate(closing[m - 2 * EPILOGUE_LAG])
+            if 0 <= m < RUNS:
                 project(m)
-            if 0 <= m - first_last < GRAPHS:
-                centre(m - first_last)
+            if m in closing:
+                centre(closing[m])

@@ -21,19 +21,16 @@ F_OUT = 512
 EPS = 1e-8
 
 PASSES = F_IN // K_PASS
-LOAD_PASSES = 8
-CHUNKS = PASSES // LOAD_PASSES
-UNITS = CHUNKS * GRAPHS
-RUN_PASSES = 4
-RUNS_PER_UNIT = LOAD_PASSES // RUN_PASSES
-RUNS = UNITS * RUNS_PER_UNIT
+CHUNK_PASSES = (4, 4, 8, 8, 8)
+CHUNK_START = tuple(sum(CHUNK_PASSES[:c]) for c in range(len(CHUNK_PASSES)))
+UNITS = len(CHUNK_PASSES) * GRAPHS
+PIECE = 4
 PAIRS = 2
 BANK_PASSES = 2
-PLANES = 4
+PLANE_PASSES = 8
 LOAD_LEAD = 3
-FLIP_LAG = 1
-PROJECT_LAG = 2
-EPILOGUE_LAG = 2
+XM_LAG = 1
+COV_LAG = 3
 
 FLOPS = 2 * GRAPHS * P * F_IN * F_OUT + 2 * GRAPHS * P * P * F_OUT
 
@@ -41,7 +38,7 @@ FLOPS = 2 * GRAPHS * P * F_IN * F_OUT + 2 * GRAPHS * P * P * F_OUT
 def tile_pearsonattention_pa_k_kernel(tc, h, W_h_words, W_h_scales, beta, out):
     nc = tc.nc
     w_words_dram = W_h_words.rearrange("g p n t -> p g (n t)").bitcast(I32)
-    w_scales_dram = W_h_scales.bitcast(I32)
+    w_scales_dram = W_h_scales.bitcast(F32)
 
     with ExitStack() as ctx:
         const = ctx.enter_context(tc.tile_pool(name="const", bufs=1))
@@ -57,10 +54,19 @@ def tile_pearsonattention_pa_k_kernel(tc, h, W_h_words, W_h_scales, beta, out):
         nc.scalar.dma_start(out=beta_bf[:], in_=beta.partition_broadcast(P))
         ident_f32 = const.tile([P, P], F32, name="ident_f32")
         make_identity(nc, ident_f32[:])
+        w_planes = []
+        for group in range(PASSES // PLANE_PASSES):
+            w_planes.append(const.tile([P, PLANE_PASSES, F_OUT], U8, name="w_planes%d" % group, align_bytes=64))
+            nc.vector.memset(w_planes[group][:].bitcast(I32), 0)
+            for quad in range(4):
+                nc.gpsimd.dma_start(
+                    out=w_planes[group][32 * quad : 32 * quad + 4, :, :].bitcast(F32),
+                    in_=w_scales_dram[
+                        group * PLANE_PASSES : (group + 1) * PLANE_PASSES, 4 * quad : 4 * quad + 4, :
+                    ].rearrange("g r n -> r g n"),
+                )
         ident_bf = const.tile([P, P], BF16, name="ident_bf")
         make_identity(nc, ident_bf[:])
-        w_planes = const.tile([P, PASSES // PLANES, F_OUT], U8, name="w_planes", align_bytes=64)
-        nc.vector.memset(w_planes[:].bitcast(I32), 0)
         one = const.tile([P, 1], F32, name="one")
         nc.vector.memset(one[:], 1.0)
         warm = const.tile([P, 1], F32, name="warm")
@@ -79,63 +85,63 @@ def tile_pearsonattention_pa_k_kernel(tc, h, W_h_words, W_h_scales, beta, out):
 
         def load(u):
             c, b = divmod(u, GRAPHS)
-            raw[u] = h_pool.tile([P, LOAD_PASSES * K_PASS], BF16, name="h_raw")
-            nc.sync.dma_start(out=raw[u][:], in_=h[b, :, c * LOAD_PASSES * K_PASS : (c + 1) * LOAD_PASSES * K_PASS])
+            first, count = CHUNK_START[c], CHUNK_PASSES[c]
+            raw[u] = h_pool.tile([P, count * K_PASS], BF16, name="h_raw")
+            nc.sync.dma_start(out=raw[u][:], in_=h[b, :, first * K_PASS : (first + count) * K_PASS])
             if b != 1:
                 return
-            for tile_no in range(c * LOAD_PASSES // PLANES, (c + 1) * LOAD_PASSES // PLANES):
-                for quad in range(4):
-                    nc.sync.dma_start(
-                        out=w_planes[32 * quad : 32 * quad + 4 * PLANES, tile_no, :].bitcast(I32),
-                        in_=w_scales_dram[PLANES * tile_no : PLANES * (tile_no + 1), 4 * quad : 4 * quad + 4, :],
-                    )
-            weights[c] = w_pool.tile([P, LOAD_PASSES, F_OUT], U32, name="w_words", align_bytes=64)
-            for g0 in range(0, LOAD_PASSES, RUN_PASSES):
+            weights[c] = w_pool.tile([P, count, F_OUT], U32, name="w_words", align_bytes=64)
+            for g0 in range(0, count, PIECE):
                 nc.sync.dma_start(
-                    out=weights[c][:, g0 : g0 + RUN_PASSES, :].bitcast(I32),
-                    in_=w_words_dram[:, c * LOAD_PASSES + g0 : c * LOAD_PASSES + g0 + RUN_PASSES, :],
+                    out=weights[c][:, g0 : g0 + PIECE, :].bitcast(I32),
+                    in_=w_words_dram[:, first + g0 : first + g0 + PIECE, :],
                 )
 
-        def sort_words(r):
-            u, part = divmod(r, RUNS_PER_UNIT)
-            ordered[r] = work.tile([P, RUN_PASSES, PAIRS, P], F32, name="h_sorted")
-            nc.vector.tensor_copy(
-                out=ordered[r][:],
-                in_=raw[u][:, part * RUN_PASSES * K_PASS : (part + 1) * RUN_PASSES * K_PASS]
-                .bitcast(F32)
-                .rearrange("n (g p i) -> n g i p", g=RUN_PASSES, i=PAIRS),
-            )
+        def sort_words(u):
+            count = CHUNK_PASSES[u // GRAPHS]
+            ordered[u] = work.tile([P, count, PAIRS, P], F32, name="h_sorted")
+            for g0 in range(0, count, PIECE):
+                nc.vector.tensor_copy(
+                    out=ordered[u][:, g0 : g0 + PIECE, :, :],
+                    in_=raw[u][:, g0 * K_PASS : (g0 + PIECE) * K_PASS]
+                    .bitcast(F32)
+                    .rearrange("n (g p i) -> n g i p", g=PIECE, i=PAIRS),
+                )
 
-        def flip_and_quantise(r):
-            grouped = work.tile([P, RUN_PASSES * K_PASS], BF16, name="h_grouped", align_bytes=64)
-            grouped_words = grouped[:].bitcast(F32).rearrange("p (g n i) -> p g n i", g=RUN_PASSES, i=PAIRS)
-            for g0 in range(0, RUN_PASSES, BANK_PASSES):
+        def flip_and_quantise(u):
+            count = CHUNK_PASSES[u // GRAPHS]
+            grouped = work.tile([P, count * K_PASS], BF16, name="h_grouped", align_bytes=64)
+            grouped_words = grouped[:].bitcast(F32).rearrange("p (g n i) -> p g n i", g=count, i=PAIRS)
+            for g0 in range(0, count, BANK_PASSES):
                 flipped = flips.tile([P, BANK_PASSES, PAIRS, P], F32, name="flipped", tag="flip")
                 for g in range(BANK_PASSES):
                     for i in range(PAIRS):
-                        nc.tensor.transpose(flipped[:, g, i, :], ordered[r][:, g0 + g, i, :], ident_f32[:])
+                        nc.tensor.transpose(flipped[:, g, i, :], ordered[u][:, g0 + g, i, :], ident_f32[:])
                 nc.scalar.copy(
                     out=grouped_words[:, g0 : g0 + BANK_PASSES, :, :],
                     in_=flipped[:].rearrange("p g i n -> p g n i"),
                 )
-            codes[r] = work.tile([P, RUN_PASSES * P], U32, name="h_codes", align_bytes=64, bufs=PROJECT_LAG + 2)
-            planes[r] = work.tile([P, RUN_PASSES * P], U8, name="h_planes", align_bytes=64, bufs=PROJECT_LAG + 2)
-            nc.vector.quantize_mx(out=codes[r][:].bitcast(FP8X4), scales=planes[r][:], in_=grouped[:])
+            codes[u] = work.tile([P, count * P], U32, name="h_codes", align_bytes=64, bufs=3)
+            planes[u] = work.tile([P, count * P], U8, name="h_planes", align_bytes=64, bufs=3)
+            for g0 in range(0, count, PIECE):
+                nc.vector.quantize_mx(
+                    out=codes[u][:, g0 * P : (g0 + PIECE) * P].bitcast(FP8X4),
+                    scales=planes[u][:, g0 * P : (g0 + PIECE) * P],
+                    in_=grouped[:, g0 * K_PASS : (g0 + PIECE) * K_PASS],
+                )
 
-        def project(r):
-            u, part = divmod(r, RUNS_PER_UNIT)
+        def project(u):
             c, b = divmod(u, GRAPHS)
-            for g in range(RUN_PASSES):
-                in_chunk = part * RUN_PASSES + g
-                tile_no, j = divmod(c * LOAD_PASSES + in_chunk, PLANES)
+            for g in range(CHUNK_PASSES[c]):
+                group, column = divmod(CHUNK_START[c] + g, PLANE_PASSES)
                 nc.tensor.matmul_mx(
                     out=acc[b][:],
-                    lhsT=codes[r][:, g * P : (g + 1) * P].bitcast(FP8X4),
-                    lhsT_scale=planes[r][:, g * P : (g + 1) * P],
-                    rhs=weights[c][:, in_chunk, :].bitcast(FP8X4),
-                    rhs_scale=w_planes[4 * j : P, tile_no, :],
-                    start=(c == 0 and in_chunk == 0),
-                    stop=(c == CHUNKS - 1 and in_chunk == LOAD_PASSES - 1),
+                    lhsT=codes[u][:, g * P : (g + 1) * P].bitcast(FP8X4),
+                    lhsT_scale=planes[u][:, g * P : (g + 1) * P],
+                    rhs=weights[c][:, g, :].bitcast(FP8X4),
+                    rhs_scale=w_planes[group][:, column, :],
+                    start=(CHUNK_START[c] + g == 0),
+                    stop=(CHUNK_START[c] + g == PASSES - 1),
                 )
 
         def centre(b):
@@ -166,6 +172,12 @@ def tile_pearsonattention_pa_k_kernel(tc, h, W_h_words, W_h_scales, beta, out):
             )
             xm_grouped = per_graph.tile([P, P, PACK], BF16, name="xm_grouped", align_bytes=64)
             nc.scalar.copy(out=xm_grouped[:], in_=xm_flipped[:].rearrange("j t n -> j n t"))
+            denom = per_graph.tile([P, P], F32, name="denom")
+            nc.vector.tensor_scalar(
+                out=denom[:], in0=norm_row[:], scalar1=t["norm"][:, 0:1], scalar2=EPS, op0=ALU.mult, op1=ALU.add
+            )
+            t["recip"] = per_graph.tile([P, P], F32, name="recip")
+            nc.vector.reciprocal(out=t["recip"][:], in_=denom[:])
             t["codes"] = per_graph.tile([P, P], U32, name="xm_codes", align_bytes=64)
             t["plane"] = per_graph.tile([P, P], U8, name="xm_plane", align_bytes=64)
             nc.vector.quantize_mx(
@@ -173,12 +185,6 @@ def tile_pearsonattention_pa_k_kernel(tc, h, W_h_words, W_h_scales, beta, out):
                 scales=t["plane"][:],
                 in_=xm_grouped[:].rearrange("j n t -> j (n t)"),
             )
-            denom = per_graph.tile([P, P], F32, name="denom")
-            nc.vector.tensor_scalar(
-                out=denom[:], in0=norm_row[:], scalar1=t["norm"][:, 0:1], scalar2=EPS, op0=ALU.mult, op1=ALU.add
-            )
-            t["recip"] = per_graph.tile([P, P], F32, name="recip")
-            nc.vector.reciprocal(out=t["recip"][:], in_=denom[:])
 
         def correlate(b):
             t = graph[b]
@@ -200,22 +206,21 @@ def tile_pearsonattention_pa_k_kernel(tc, h, W_h_words, W_h_scales, beta, out):
             )
             nc.sync.dma_start(out=out[b], in_=result[:])
 
-        closing = {(UNITS - GRAPHS + b + 1) * RUNS_PER_UNIT - 1: b for b in range(GRAPHS)}
-        sort_lag = LOAD_LEAD * RUNS_PER_UNIT
-        for step in range(RUNS + sort_lag + FLIP_LAG + PROJECT_LAG + 2 * EPILOGUE_LAG):
-            if step % RUNS_PER_UNIT == 0 and step < RUNS:
-                load(step // RUNS_PER_UNIT)
-            r = step - sort_lag
-            if 0 <= r < RUNS:
-                sort_words(r)
-            if 0 <= r - FLIP_LAG < RUNS:
-                flip_and_quantise(r - FLIP_LAG)
-            m = r - FLIP_LAG - PROJECT_LAG
-            if m - EPILOGUE_LAG in closing:
-                flip_xm(closing[m - EPILOGUE_LAG])
-            if m - 2 * EPILOGUE_LAG in closing:
-                correlate(closing[m - 2 * EPILOGUE_LAG])
-            if 0 <= m < RUNS:
-                project(m)
-            if m in closing:
-                centre(closing[m])
+        first_closing = UNITS - GRAPHS
+        for step in range(UNITS + LOAD_LEAD + 2 + COV_LAG):
+            if step < UNITS:
+                load(step)
+            u = step - LOAD_LEAD
+            if 0 <= u < UNITS:
+                sort_words(u)
+            if 0 <= u - 1 < UNITS:
+                flip_and_quantise(u - 1)
+            closed = u - 2 - first_closing
+            if 0 <= u - 2 < UNITS:
+                project(u - 2)
+            if 0 <= closed < GRAPHS:
+                centre(closed)
+            if 0 <= closed - XM_LAG < GRAPHS:
+                flip_xm(closed - XM_LAG)
+            if 0 <= closed - COV_LAG < GRAPHS:
+                correlate(closed - COV_LAG)

@@ -58,7 +58,7 @@ def tile_pearsonattention_pa_k_kernel(tc, h, W_h_words, W_h_scales, beta, out):
         for group in range(PASSES // PLANE_PASSES):
             w_planes.append(const.tile([P, PLANE_PASSES, F_OUT], U8, name="w_planes%d" % group, align_bytes=64))
             nc.vector.memset(w_planes[group][:].bitcast(I32), 0)
-            for quad in range(4):
+            for quad in range(4 if group > 0 else 0):
                 nc.gpsimd.dma_start(
                     out=w_planes[group][32 * quad : 32 * quad + 4, :, :].bitcast(F32),
                     in_=w_scales_dram[
@@ -72,7 +72,6 @@ def tile_pearsonattention_pa_k_kernel(tc, h, W_h_words, W_h_scales, beta, out):
         warm = const.tile([P, 1], F32, name="warm")
         nc.scalar.activation(out=warm[:], in_=one[:], func=ACT.Sqrt)
         beta_f32 = const.tile([P, 1], F32, name="beta_f32")
-        nc.vector.tensor_copy(out=beta_f32[:], in_=beta_bf[:])
 
         acc = [sums.tile([P, F_OUT], F32, name="acc%d" % b) for b in range(GRAPHS)]
 
@@ -88,6 +87,14 @@ def tile_pearsonattention_pa_k_kernel(tc, h, W_h_words, W_h_scales, beta, out):
             first, count = CHUNK_START[c], CHUNK_PASSES[c]
             raw[u] = h_pool.tile([P, count * K_PASS], BF16, name="h_raw")
             nc.sync.dma_start(out=raw[u][:], in_=h[b, :, first * K_PASS : (first + count) * K_PASS])
+            if u == 0:
+                for quad in range(4):
+                    nc.sync.dma_start(
+                        out=w_planes[0][32 * quad : 32 * quad + 4, :, :].bitcast(I32),
+                        in_=W_h_scales.bitcast(I32)[0:PLANE_PASSES, 4 * quad : 4 * quad + 4, :].rearrange(
+                            "g r n -> r g n"
+                        ),
+                    )
             if b != 1:
                 return
             weights[c] = w_pool.tile([P, count, F_OUT], U32, name="w_words", align_bytes=64)
@@ -213,6 +220,8 @@ def tile_pearsonattention_pa_k_kernel(tc, h, W_h_words, W_h_scales, beta, out):
             u = step - LOAD_LEAD
             if 0 <= u < UNITS:
                 sort_words(u)
+            if u == 1:
+                nc.vector.tensor_copy(out=beta_f32[:], in_=beta_bf[:])
             if 0 <= u - 1 < UNITS:
                 flip_and_quantise(u - 1)
             closed = u - 2 - first_closing

@@ -29,8 +29,9 @@ PAIRS = 2
 BANK_PASSES = 2
 PLANE_PASSES = 8
 LOAD_LEAD = 3
-XM_LAG = 1
-COV_LAG = 3
+NORM_LAG = 1
+XM_LAG = 3
+COV_LAG = 6
 
 FLOPS = 2 * GRAPHS * P * F_IN * F_OUT + 2 * GRAPHS * P * P * F_OUT
 
@@ -165,8 +166,12 @@ def tile_pearsonattention_pa_k_kernel(tc, h, W_h_words, W_h_scales, beta, out):
                 scalar2=None,
                 op0=ALU.subtract,
             )
+            t["mean_var"] = mean_var
+
+        def norm_of(b):
+            t = graph[b]
             t["norm"] = per_graph.tile([P, 1], F32, name="norm")
-            nc.scalar.activation(out=t["norm"][:], in_=mean_var[:, 1:2], func=ACT.Sqrt, scale=float(F_OUT))
+            nc.scalar.activation(out=t["norm"][:], in_=t["mean_var"][:, 1:2], func=ACT.Sqrt, scale=float(F_OUT))
 
         def flip_xm(b):
             t = graph[b]
@@ -174,17 +179,11 @@ def tile_pearsonattention_pa_k_kernel(tc, h, W_h_words, W_h_scales, beta, out):
             for k in range(PACK):
                 nc.tensor.transpose(xm_flipped[:, k, :], t["xm"][:, k, :], ident_bf[:])
             norm_row = flips.tile([P, P], F32, name="norm_row", tag="flip")
-            nc.tensor.matmul(
-                out=norm_row[:], lhsT=t["norm"][:, 0:1].to_broadcast([P, P]), rhs=ident_f32[:], start=True, stop=True
-            )
+            nc.tensor.transpose(norm_row[:], t["norm"][:, 0:1].to_broadcast([P, P]), ident_f32[:])
             xm_grouped = per_graph.tile([P, P, PACK], BF16, name="xm_grouped", align_bytes=64)
             nc.scalar.copy(out=xm_grouped[:], in_=xm_flipped[:].rearrange("j t n -> j n t"))
             denom = per_graph.tile([P, P], F32, name="denom")
-            nc.vector.tensor_scalar(
-                out=denom[:], in0=norm_row[:], scalar1=t["norm"][:, 0:1], scalar2=EPS, op0=ALU.mult, op1=ALU.add
-            )
-            t["recip"] = per_graph.tile([P, P], F32, name="recip")
-            nc.vector.reciprocal(out=t["recip"][:], in_=denom[:])
+            nc.scalar.activation(out=denom[:], in_=norm_row[:], func=ACT.Copy, scale=t["norm"][:, 0:1], bias=EPS)
             t["codes"] = per_graph.tile([P, P], U32, name="xm_codes", align_bytes=64)
             t["plane"] = per_graph.tile([P, P], U8, name="xm_plane", align_bytes=64)
             nc.vector.quantize_mx(
@@ -192,6 +191,8 @@ def tile_pearsonattention_pa_k_kernel(tc, h, W_h_words, W_h_scales, beta, out):
                 scales=t["plane"][:],
                 in_=xm_grouped[:].rearrange("j n t -> j (n t)"),
             )
+            t["recip"] = per_graph.tile([P, P], F32, name="recip")
+            nc.vector.reciprocal(out=t["recip"][:], in_=denom[:])
 
         def correlate(b):
             t = graph[b]
@@ -229,6 +230,8 @@ def tile_pearsonattention_pa_k_kernel(tc, h, W_h_words, W_h_scales, beta, out):
                 project(u - 2)
             if 0 <= closed < GRAPHS:
                 centre(closed)
+            if 0 <= closed - NORM_LAG < GRAPHS:
+                norm_of(closed - NORM_LAG)
             if 0 <= closed - XM_LAG < GRAPHS:
                 flip_xm(closed - XM_LAG)
             if 0 <= closed - COV_LAG < GRAPHS:

@@ -28,6 +28,7 @@ PIECE = 4
 PAIRS = 2
 BANK_PASSES = 2
 PLANE_PASSES = 8
+PLANE_SHARE = 4
 LOAD_LEAD = 3
 NORM_LAG = 1
 XM_LAG = 3
@@ -39,7 +40,6 @@ FLOPS = 2 * GRAPHS * P * F_IN * F_OUT + 2 * GRAPHS * P * P * F_OUT
 def tile_pearsonattention_pa_k_kernel(tc, h, W_h_words, W_h_scales, beta, out):
     nc = tc.nc
     w_words_dram = W_h_words.rearrange("g p n t -> p g (n t)").bitcast(I32)
-    w_scales_dram = W_h_scales.bitcast(F32)
 
     with ExitStack() as ctx:
         const = ctx.enter_context(tc.tile_pool(name="const", bufs=1))
@@ -57,15 +57,24 @@ def tile_pearsonattention_pa_k_kernel(tc, h, W_h_words, W_h_scales, beta, out):
         make_identity(nc, ident_f32[:])
         w_planes = []
         for group in range(PASSES // PLANE_PASSES):
-            w_planes.append(const.tile([P, PLANE_PASSES, F_OUT], U8, name="w_planes%d" % group, align_bytes=64))
+            w_planes.append(
+                const.tile([P, PLANE_PASSES // PLANE_SHARE, F_OUT], U8, name="w_planes%d" % group, align_bytes=64)
+            )
             nc.vector.memset(w_planes[group][:].bitcast(I32), 0)
-            for quad in range(4 if group > 0 else 0):
-                nc.gpsimd.dma_start(
-                    out=w_planes[group][32 * quad : 32 * quad + 4, :, :].bitcast(F32),
-                    in_=w_scales_dram[
-                        group * PLANE_PASSES : (group + 1) * PLANE_PASSES, 4 * quad : 4 * quad + 4, :
-                    ].rearrange("g r n -> r g n"),
-                )
+
+        def load_planes(queue, word, c):
+            for g0 in range(CHUNK_START[c], CHUNK_START[c] + CHUNK_PASSES[c], PLANE_SHARE):
+                group, place = divmod(g0, PLANE_PASSES)
+                for quad in range(4):
+                    queue.dma_start(
+                        out=w_planes[group][
+                            32 * quad : 32 * quad + 4 * PLANE_SHARE, place // PLANE_SHARE, :
+                        ].bitcast(word),
+                        in_=W_h_scales.bitcast(word)[g0 : g0 + PLANE_SHARE, 4 * quad : 4 * quad + 4, :],
+                    )
+
+        for c in range(1, len(CHUNK_PASSES)):
+            load_planes(nc.gpsimd, F32, c)
         ident_bf = const.tile([P, P], BF16, name="ident_bf")
         make_identity(nc, ident_bf[:])
         one = const.tile([P, 1], F32, name="one")
@@ -89,13 +98,7 @@ def tile_pearsonattention_pa_k_kernel(tc, h, W_h_words, W_h_scales, beta, out):
             raw[u] = h_pool.tile([P, count * K_PASS], BF16, name="h_raw")
             nc.sync.dma_start(out=raw[u][:], in_=h[b, :, first * K_PASS : (first + count) * K_PASS])
             if u == 0:
-                for quad in range(4):
-                    nc.sync.dma_start(
-                        out=w_planes[0][32 * quad : 32 * quad + 4, :, :].bitcast(I32),
-                        in_=W_h_scales.bitcast(I32)[0:PLANE_PASSES, 4 * quad : 4 * quad + 4, :].rearrange(
-                            "g r n -> r g n"
-                        ),
-                    )
+                load_planes(nc.sync, I32, 0)
             if b != 1:
                 return
             weights[c] = w_pool.tile([P, count, F_OUT], U32, name="w_words", align_bytes=64)
@@ -141,13 +144,14 @@ def tile_pearsonattention_pa_k_kernel(tc, h, W_h_words, W_h_scales, beta, out):
         def project(u):
             c, b = divmod(u, GRAPHS)
             for g in range(CHUNK_PASSES[c]):
-                group, column = divmod(CHUNK_START[c] + g, PLANE_PASSES)
+                group, place = divmod(CHUNK_START[c] + g, PLANE_PASSES)
+                column, share = divmod(place, PLANE_SHARE)
                 nc.tensor.matmul_mx(
                     out=acc[b][:],
                     lhsT=codes[u][:, g * P : (g + 1) * P].bitcast(FP8X4),
                     lhsT_scale=planes[u][:, g * P : (g + 1) * P],
                     rhs=weights[c][:, g, :].bitcast(FP8X4),
-                    rhs_scale=w_planes[group][:, column, :],
+                    rhs_scale=w_planes[group][4 * share : P, column, :],
                     start=(CHUNK_START[c] + g == 0),
                     stop=(CHUNK_START[c] + g == PASSES - 1),
                 )

@@ -52,7 +52,6 @@ def tile_pearsonattention_pa_k_kernel(tc, h, W_h_words, W_h_scales, beta, out):
         ctx.enter_context(tc.manual_schedule())
 
         beta_bf = const.tile([P, 1], BF16, name="beta_bf")
-        nc.scalar.dma_start(out=beta_bf[:], in_=beta.partition_broadcast(P))
         ident_f32 = const.tile([P, P], F32, name="ident_f32")
         make_identity(nc, ident_f32[:])
         w_planes = []
@@ -81,7 +80,6 @@ def tile_pearsonattention_pa_k_kernel(tc, h, W_h_words, W_h_scales, beta, out):
         nc.vector.memset(one[:], 1.0)
         warm = const.tile([P, 1], F32, name="warm")
         nc.scalar.activation(out=warm[:], in_=one[:], func=ACT.Sqrt)
-        beta_f32 = const.tile([P, 1], F32, name="beta_f32")
 
         acc = [sums.tile([P, F_OUT], F32, name="acc%d" % b) for b in range(GRAPHS)]
 
@@ -99,6 +97,8 @@ def tile_pearsonattention_pa_k_kernel(tc, h, W_h_words, W_h_scales, beta, out):
             nc.sync.dma_start(out=raw[u][:], in_=h[b, :, first * K_PASS : (first + count) * K_PASS])
             if u == 0:
                 load_planes(nc.sync, I32, 0)
+            if u == UNITS - 1:
+                nc.sync.dma_start(out=beta_bf[:], in_=beta.partition_broadcast(P))
             if b != 1:
                 return
             weights[c] = w_pool.tile([P, count, F_OUT], U32, name="w_words", align_bytes=64)
@@ -214,7 +214,7 @@ def tile_pearsonattention_pa_k_kernel(tc, h, W_h_words, W_h_scales, beta, out):
             nc.scalar.activation(out=cov_abs[:], in_=cov[:], func=ACT.Abs)
             result = per_graph.tile([P, P], F32, name="result")
             nc.vector.scalar_tensor_tensor(
-                out=result[:], in0=cov_abs[:], scalar=beta_f32[:, 0:1], in1=t["recip"][:], op0=ALU.mult, op1=ALU.mult
+                out=result[:], in0=cov_abs[:], scalar=beta_bf[:, 0:1], in1=t["recip"][:], op0=ALU.mult, op1=ALU.mult
             )
             nc.sync.dma_start(out=out[b], in_=result[:])
 
@@ -225,8 +225,6 @@ def tile_pearsonattention_pa_k_kernel(tc, h, W_h_words, W_h_scales, beta, out):
             u = step - LOAD_LEAD
             if 0 <= u < UNITS:
                 sort_words(u)
-            if u == 1:
-                nc.vector.tensor_copy(out=beta_f32[:], in_=beta_bf[:])
             if 0 <= u - 1 < UNITS:
                 flip_and_quantise(u - 1)
             closed = u - 2 - first_closing

from contextlib import ExitStack

import concourse.mybir as mybir
from concourse.masks import make_identity

F32 = mybir.dt.float32
BF16 = mybir.dt.bfloat16
I32 = mybir.dt.int32
U32 = mybir.dt.uint32
U8 = mybir.dt.uint8
FP8X4 = mybir.dt.float8_e4m3fn_x4
ACT = mybir.ActivationFunctionType
ALU = mybir.AluOpType

P = 128
PACK = 4
K_PASS = P * PACK
GRAPHS = 4
F_IN = 16384
F_OUT = 512
EPS = 1e-8

PASSES = F_IN // K_PASS
CHUNK_PASSES = (4, 4, 8, 8, 8)
CHUNK_START = tuple(sum(CHUNK_PASSES[:c]) for c in range(len(CHUNK_PASSES)))
UNITS = len(CHUNK_PASSES) * GRAPHS
PIECE = 4
PAIRS = 2
BANK_PASSES = 2
PLANE_PASSES = 8
PLANE_SHARE = 4
LOAD_LEAD = 3
NORM_LAG = 1
XM_LAG = 3
COV_LAG = 6

FLOPS = 2 * GRAPHS * P * F_IN * F_OUT + 2 * GRAPHS * P * P * F_OUT


def tile_pearsonattention_pa_k_kernel(tc, h, W_h_words, W_h_scales, beta, out):
    nc = tc.nc
    w_words_dram = W_h_words.rearrange("g p n t -> p g (n t)").bitcast(I32)

    with ExitStack() as ctx:
        const = ctx.enter_context(tc.tile_pool(name="const", bufs=1))
        h_pool = ctx.enter_context(tc.tile_pool(name="h_pool", bufs=LOAD_LEAD + 1))
        w_pool = ctx.enter_context(tc.tile_pool(name="w_pool", bufs=2))
        work = ctx.enter_context(tc.tile_pool(name="work", bufs=2))
        per_graph = ctx.enter_context(tc.tile_pool(name="per_graph", bufs=GRAPHS))
        sums = ctx.enter_context(tc.psum_pool(name="sums", bufs=1))
        flips = ctx.enter_context(tc.psum_pool(name="flips", bufs=4))
        ctx.enter_context(tc.manual_schedule())

        beta_bf = const.tile([P, 1], BF16, name="beta_bf")
        ident_f32 = const.tile([P, P], F32, name="ident_f32")
        make_identity(nc, ident_f32[:])
        w_planes = []
        for group in range(PASSES // PLANE_PASSES):
            w_planes.append(
                const.tile([P, PLANE_PASSES // PLANE_SHARE, F_OUT], U8, name="w_planes%d" % group, align_bytes=64)
            )
            nc.vector.memset(w_planes[group][:].bitcast(I32), 0)

        def load_planes(queue, word, c):
            for g0 in range(CHUNK_START[c], CHUNK_START[c] + CHUNK_PASSES[c], PLANE_SHARE):
                group, place = divmod(g0, PLANE_PASSES)
                for quad in range(4):
                    queue.dma_start(
                        out=w_planes[group][
                            32 * quad : 32 * quad + 4 * PLANE_SHARE, place // PLANE_SHARE, :
                        ].bitcast(word),
                        in_=W_h_scales.bitcast(word)[g0 : g0 + PLANE_SHARE, 4 * quad : 4 * quad + 4, :],
                    )

        for c in range(1, len(CHUNK_PASSES)):
            load_planes(nc.gpsimd, F32, c)
        ident_bf = const.tile([P, P], BF16, name="ident_bf")
        make_identity(nc, ident_bf[:])
        one = const.tile([P, 1], F32, name="one")
        nc.vector.memset(one[:], 1.0)
        warm = const.tile([P, 1], F32, name="warm")
        nc.scalar.activation(out=warm[:], in_=one[:], func=ACT.Sqrt)

        acc = [sums.tile([P, F_OUT], F32, name="acc%d" % b) for b in range(GRAPHS)]

        raw = {}
        weights = {}
        ordered = {}
        codes = {}
        planes = {}
        graph = [{} for b in range(GRAPHS)]

        def load(u):
            c, b = divmod(u, GRAPHS)
            first, count = CHUNK_START[c], CHUNK_PASSES[c]
            raw[u] = h_pool.tile([P, count * K_PASS], BF16, name="h_raw")
            nc.sync.dma_start(out=raw[u][:], in_=h[b, :, first * K_PASS : (first + count) * K_PASS])
            if u == 0:
                load_planes(nc.sync, I32, 0)
            if u == UNITS - 1:
                nc.sync.dma_start(out=beta_bf[:], in_=beta.partition_broadcast(P))
            if b != 1:
                return
            weights[c] = w_pool.tile([P, count, F_OUT], U32, name="w_words", align_bytes=64)
            for g0 in range(0, count, PIECE):
                nc.sync.dma_start(
                    out=weights[c][:, g0 : g0 + PIECE, :].bitcast(I32),
                    in_=w_words_dram[:, first + g0 : first + g0 + PIECE, :],
                )

        def sort_words(u):
            count = CHUNK_PASSES[u // GRAPHS]
            ordered[u] = work.tile([P, count, PAIRS, P], F32, name="h_sorted")
            for g0 in range(0, count, PIECE):
                nc.vector.tensor_copy(
                    out=ordered[u][:, g0 : g0 + PIECE, :, :],
                    in_=raw[u][:, g0 * K_PASS : (g0 + PIECE) * K_PASS]
                    .bitcast(F32)
                    .rearrange("n (g p i) -> n g i p", g=PIECE, i=PAIRS),
                )

        def flip_and_quantise(u):
            count = CHUNK_PASSES[u // GRAPHS]
            grouped = work.tile([P, count * K_PASS], BF16, name="h_grouped", align_bytes=64)
            grouped_words = grouped[:].bitcast(F32).rearrange("p (g n i) -> p g n i", g=count, i=PAIRS)
            for g0 in range(0, count, BANK_PASSES):
                flipped = flips.tile([P, BANK_PASSES, PAIRS, P], F32, name="flipped", tag="flip")
                for g in range(BANK_PASSES):
                    for i in range(PAIRS):
                        nc.tensor.transpose(flipped[:, g, i, :], ordered[u][:, g0 + g, i, :], ident_f32[:])
                nc.scalar.copy(
                    out=grouped_words[:, g0 : g0 + BANK_PASSES, :, :],
                    in_=flipped[:].rearrange("p g i n -> p g n i"),
                )
            codes[u] = work.tile([P, count * P], U32, name="h_codes", align_bytes=64, bufs=3)
            planes[u] = work.tile([P, count * P], U8, name="h_planes", align_bytes=64, bufs=3)
            for g0 in range(0, count, PIECE):
                nc.vector.quantize_mx(
                    out=codes[u][:, g0 * P : (g0 + PIECE) * P].bitcast(FP8X4),
                    scales=planes[u][:, g0 * P : (g0 + PIECE) * P],
                    in_=grouped[:, g0 * K_PASS : (g0 + PIECE) * K_PASS],
                )

        def project(u):
            c, b = divmod(u, GRAPHS)
            for g in range(CHUNK_PASSES[c]):
                group, place = divmod(CHUNK_START[c] + g, PLANE_PASSES)
                column, share = divmod(place, PLANE_SHARE)
                nc.tensor.matmul_mx(
                    out=acc[b][:],
                    lhsT=codes[u][:, g * P : (g + 1) * P].bitcast(FP8X4),
                    lhsT_scale=planes[u][:, g * P : (g + 1) * P],
                    rhs=weights[c][:, g, :].bitcast(FP8X4),
                    rhs_scale=w_planes[group][4 * share : P, column, :],
                    start=(CHUNK_START[c] + g == 0),
                    stop=(CHUNK_START[c] + g == PASSES - 1),
                )

        def centre(b):
            t = graph[b]
            stats = per_graph.tile([P, 6], F32, name="stats")
            nc.vector.bn_stats(out=stats[:], in_=acc[b][:])
            mean_var = per_graph.tile([P, 2], F32, name="mean_var")
            nc.vector.bn_aggr(out=mean_var[:], in_=stats[:])
            t["xm"] = per_graph.tile([P, PACK, P], BF16, name="xm")
            nc.vector.tensor_scalar(
                out=t["xm"][:],
                in0=acc[b][:].rearrange("n (j t) -> n t j", t=PACK),
                scalar1=mean_var[:, 0:1],
                scalar2=None,
                op0=ALU.subtract,
            )
            t["mean_var"] = mean_var

        def norm_of(b):
            t = graph[b]
            t["norm"] = per_graph.tile([P, 1], F32, name="norm")
            nc.scalar.activation(out=t["norm"][:], in_=t["mean_var"][:, 1:2], func=ACT.Sqrt, scale=float(F_OUT))

        def flip_xm(b):
            t = graph[b]
            xm_flipped = sums.tile([P, PACK, P], BF16, name="xm_flipped", tag="acc%d" % b)
            for k in range(PACK):
                nc.tensor.transpose(xm_flipped[:, k, :], t["xm"][:, k, :], ident_bf[:])
            norm_row = flips.tile([P, P], F32, name="norm_row", tag="flip")
            nc.tensor.transpose(norm_row[:], t["norm"][:, 0:1].to_broadcast([P, P]), ident_f32[:])
            xm_grouped = per_graph.tile([P, P, PACK], BF16, name="xm_grouped", align_bytes=64)
            nc.scalar.copy(out=xm_grouped[:], in_=xm_flipped[:].rearrange("j t n -> j n t"))
            denom = per_graph.tile([P, P], F32, name="denom")
            nc.scalar.activation(out=denom[:], in_=norm_row[:], func=ACT.Copy, scale=t["norm"][:, 0:1], bias=EPS)
            t["codes"] = per_graph.tile([P, P], U32, name="xm_codes", align_bytes=64)
            t["plane"] = per_graph.tile([P, P], U8, name="xm_plane", align_bytes=64)
            nc.vector.quantize_mx(
                out=t["codes"][:].bitcast(FP8X4),
                scales=t["plane"][:],
                in_=xm_grouped[:].rearrange("j n t -> j (n t)"),
            )
            t["recip"] = per_graph.tile([P, P], F32, name="recip")
            nc.vector.reciprocal(out=t["recip"][:], in_=denom[:])

        def correlate(b):
            t = graph[b]
            cov = sums.tile([P, P], F32, name="cov", tag="acc%d" % b)
            nc.tensor.matmul_mx(
                out=cov[:],
                lhsT=t["codes"][:].bitcast(FP8X4),
                lhsT_scale=t["plane"][:],
                rhs=t["codes"][:].bitcast(FP8X4),
                rhs_scale=t["plane"][:],
                start=True,
                stop=True,
            )
            cov_abs = per_graph.tile([P, P], F32, name="cov_abs")
            nc.scalar.activation(out=cov_abs[:], in_=cov[:], func=ACT.Abs)
            result = per_graph.tile([P, P], F32, name="result")
            nc.vector.scalar_tensor_tensor(
                out=result[:], in0=cov_abs[:], scalar=beta_bf[:, 0:1], in1=t["recip"][:], op0=ALU.mult, op1=ALU.mult
            )
            nc.sync.dma_start(out=out[b], in_=result[:])

        first_closing = UNITS - GRAPHS
        for step in range(UNITS + LOAD_LEAD + 2 + COV_LAG):
            if step < UNITS:
                load(step)
            u = step - LOAD_LEAD
            if 0 <= u < UNITS:
                sort_words(u)
            if 0 <= u - 1 < UNITS:
                flip_and_quantise(u - 1)
            closed = u - 2 - first_closing
            if 0 <= u - 2 < UNITS:
                project(u - 2)
            if 0 <= closed < GRAPHS:
                centre(closed)
            if 0 <= closed - NORM_LAG < GRAPHS:
                norm_of(closed - NORM_LAG)
            if 0 <= closed - XM_LAG < GRAPHS:
                flip_xm(closed - XM_LAG)
            if 0 <= closed - COV_LAG < GRAPHS:
                correlate(closed - COV_LAG)
